import numpy as np
import ml_dtypes


def mxq(x, axis, fmt="e4m3"):
    dtype, down = {"e4m3": (ml_dtypes.float8_e4m3fn, 7), "e5m2": (ml_dtypes.float8_e5m2, 14)}[fmt]
    v = np.moveaxis(np.asarray(x, np.float32).astype(ml_dtypes.bfloat16).astype(np.float64), axis, -1)
    blocks = v.reshape(v.shape[:-1] + (-1, 32))
    amax = np.abs(blocks).max(-1, keepdims=True)
    byte = np.maximum(np.where(amax > 0, np.frexp(amax)[1] - 1 + 127, 0) - down, 1)
    scale = np.exp2(byte - 127.0)
    codes = (blocks / scale).astype(np.float32).astype(dtype).astype(np.float64)
    return np.moveaxis((codes * scale).reshape(v.shape), -1, axis)


WIDE = False


def mx_kscale(k):
    if not WIDE:
        return np.ones(k)
    levels = np.array([10, -10, 5, -5, 0])
    a = np.random.permutation(np.resize(levels, k // 512 * 4)).reshape(k // 512, 4)
    idx = np.arange(k)
    return np.exp2(a[idx // 512, idx % 128 // 32])


BF16 = ml_dtypes.bfloat16


def bf(x):
    return np.asarray(x, np.float32).astype(BF16)


def f64(x):
    return np.asarray(x).astype(np.float64)


E2M1 = np.array([0.0, 0.5, 1.0, 1.5, 2.0, 3.0, 4.0, 6.0, -0.0, -0.5, -1.0, -1.5, -2.0, -3.0, -4.0, -6.0])


def pack_weight(w, fmt):
    k, n = w.shape
    w = f64(bf(w)).reshape(k // 32, 32, n)
    amax = np.abs(w).max(1)
    if fmt == "e4m3":
        byte = np.frexp(amax)[1] - 1 + 127 - 7
    else:
        mant, ex = np.frexp(amax / 6.0)
        byte = np.where(mant > 0.5, ex, ex - 1) + 127
    byte = np.clip(np.where(amax > 0, byte, 1), 1, 254)
    scaled = (w * np.exp2(127.0 - byte)[:, None, :]).reshape(k, n).astype(np.float32)
    by_word = np.ascontiguousarray(scaled.reshape(k // 512, 128, 4, n).transpose(0, 1, 3, 2))
    if fmt == "e4m3":
        words = by_word.astype(ml_dtypes.float8_e4m3fn).view(np.uint8)
    else:
        c = by_word.astype(ml_dtypes.float4_e2m1fn).view(np.uint8) & 0xF
        words = c[..., 0::2] | (c[..., 1::2] << 4)
    return np.ascontiguousarray(words), np.ascontiguousarray(byte.astype(np.uint8).reshape(k // 512, 16, n))


def unpack_weight(words, scales, fmt):
    g, p, n, _ = words.shape
    if fmt == "e4m3":
        vals = np.ascontiguousarray(words).view(ml_dtypes.float8_e4m3fn).astype(np.float64)
    else:
        nib = np.empty((g, p, n, 4), np.uint8)
        nib[..., 0::2] = words & 0xF
        nib[..., 1::2] = words >> 4
        vals = E2M1[nib]
    vals = vals * np.repeat(np.exp2(scales.astype(np.float64) - 127.0), 8, axis=1)[..., None]
    return vals.transpose(0, 1, 3, 2).reshape(g * 512, n)

def pack4(w):
    words, scales = pack_weight(w, "e2m1")
    return words.reshape(words.shape[0], 128, -1), scales


def unpack4(words, scales):
    return unpack_weight(words.reshape(words.shape[0], 128, -1, 2), scales, "e2m1")


B, F, H, E = 256, 128, 512, 128


def setup_inputs():
    t = mx_kscale(H)
    x = bf(np.random.standard_normal((B, F)))
    w1 = bf(np.random.uniform(-1.0, 1.0, (F, H)) * t)
    b1 = bf(np.random.uniform(-1.0, 1.0, (F, H)) * t)
    w2 = np.random.standard_normal((F, H, E)) * 1.5 / np.sqrt(H) / t[None, :, None]
    w2_words, w2_scales = pack4(w2.reshape(-1, E))
    b2 = bf(np.random.standard_normal((F, E)) * 0.3)
    return {"x": x,
            "w1": w1,
            "b1": b1,
            "w2_words": w2_words,
            "w2_scales": w2_scales,
            "b2": b2}


def reference(x, w1, b1, w2_words, w2_scales, b2):
    h = np.maximum(f64(x)[:, :, None] * f64(w1)[None] + f64(b1)[None], 0.0)
    hq = mxq(h, 2, "e4m3")
    out = (hq.transpose(1, 0, 2) @ unpack4(w2_words, w2_scales).reshape(F, H, E)).transpose(1, 0, 2) + f64(b2)[None]
    return out.reshape(x.shape[0], F * E)

@@ -1,0 +1,140 @@
+from contextlib import ExitStack
+
+import concourse.mybir as mybir
+from concourse.masks import make_identity
+
+BF16 = mybir.dt.bfloat16
+F32 = mybir.dt.float32
+I32 = mybir.dt.int32
+U8 = mybir.dt.uint8
+U32 = mybir.dt.uint32
+FP8X4 = mybir.dt.float8_e4m3fn_x4
+FP4X4 = mybir.dt.float4_e2m1fn_x4
+ALU = mybir.AluOpType
+ACT = mybir.ActivationFunctionType
+
+P = 128
+B, F, H, E = 256, 128, 512, 128
+PACK = 4
+HALVES = B // P
+GROUP = 4
+CHUNK = 16
+RUN = 4
+SCALAR_COLS = GROUP * B * 7 // 8
+
+FLOPS = 2 * B * F * H * E
+
+
+def transposed_scalars(nc, psum, pool, rows, ident, name):
+    turned = psum.tile([P, PACK, F], BF16, name=name + "_ps")
+    for t in range(PACK):
+        nc.tensor.transpose(turned[:, t, :], rows[:, t:H:PACK], ident)
+    scalars = pool.tile([P, PACK, F], F32, name=name)
+    nc.vector.tensor_copy(out=scalars[:], in_=turned[:])
+    return scalars
+
+
+def tile_densefeaturenumericembedding_e_kernel(tc, x, w1, b1, w2_words, w2_scales, b2, out):
+    nc = tc.nc
+    with ExitStack() as ctx:
+        const = ctx.enter_context(tc.tile_pool(name="const", bufs=1))
+        xpool = ctx.enter_context(tc.tile_pool(name="xpool", bufs=3))
+        work = ctx.enter_context(tc.tile_pool(name="work", bufs=3))
+        opool = ctx.enter_context(tc.tile_pool(name="opool", bufs=4))
+        setup_psum = ctx.enter_context(tc.psum_pool(name="setup_psum", bufs=1))
+        psum = ctx.enter_context(tc.psum_pool(name="psum", bufs=4))
+
+        x_sb = const.tile([P, HALVES, F], BF16)
+        nc.sync.dma_start(out=x_sb[:], in_=x.rearrange("(h p) f -> p h f", p=P))
+        w1_sb = const.tile([P, H], BF16)
+        nc.sync.dma_start(out=w1_sb[:], in_=w1)
+        b1_sb = const.tile([P, H], BF16)
+        nc.sync.dma_start(out=b1_sb[:], in_=b1)
+
+        ident = const.tile([P, P], BF16)
+        make_identity(nc, ident[:])
+
+        w2_planes = const.tile([P, F, E], U8, align_bytes=64)
+        nc.vector.memset(w2_planes[:].rearrange("p g n -> p (g n)").bitcast(I32), 0)
+
+        xT_ps = setup_psum.tile([P, B], BF16)
+        for h in range(HALVES):
+            nc.tensor.transpose(xT_ps[:, h * P : (h + 1) * P], x_sb[:, h, :], ident[:])
+        xT_sb = const.tile([P, B], BF16)
+        nc.vector.tensor_copy(out=xT_sb[:], in_=xT_ps[:])
+        nc.sync.dma_start(
+            out=out[0:1, :].rearrange("o (f w) -> (o f) w", w=B // 2), in_=xT_sb[:].bitcast(F32)
+        )
+
+        w1T = transposed_scalars(nc, setup_psum, const, w1_sb, ident[:], "w1T")
+        b1T = transposed_scalars(nc, setup_psum, const, b1_sb, ident[:], "b1T")
+
+        for q in range(4):
+            nc.sync.dma_start(
+                out=w2_planes[32 * q : 32 * q + 4, :, :].bitcast(I32),
+                in_=w2_scales[:, 4 * q : 4 * q + 4, :].bitcast(I32).rearrange("g r n -> r g n"),
+            )
+        w2_codes = const.tile([P, F, 2 * E], U8, align_bytes=64)
+        b2_all = const.tile([P, F * E], BF16)
+        b2_row = b2.rearrange("f e -> (f e)")
+
+        words = CHUNK * B // 2
+        for c in range(F // CHUNK):
+            feats = slice(c * CHUNK, (c + 1) * CHUNK)
+            xb = xpool.tile([P, words], F32)
+            nc.sync.dma_start(out=xb[:], in_=out[0, c * words : (c + 1) * words].partition_broadcast(P))
+            nc.sync.dma_start(
+                out=w2_codes[:, feats, :].bitcast(I32),
+                in_=w2_words[feats].bitcast(I32).rearrange("g p w -> p g w"),
+            )
+            nc.sync.dma_start(
+                out=b2_all[:, c * CHUNK * E : (c + 1) * CHUNK * E],
+                in_=b2_row[c * CHUNK * E : (c + 1) * CHUNK * E].partition_broadcast(P),
+            )
+            x_all = xb[:].bitcast(BF16)
+
+            for g in range(CHUNK // GROUP):
+                f0 = c * CHUNK + g * GROUP
+                pre = work.tile([P, PACK, GROUP * B], BF16)
+                for j in range(GROUP):
+                    for t in range(PACK):
+                        nc.vector.tensor_scalar(
+                            out=pre[:, t, j * B : (j + 1) * B],
+                            in0=x_all[:, (g * GROUP + j) * B : (g * GROUP + j + 1) * B],
+                            scalar1=w1T[:, t, f0 + j : f0 + j + 1],
+                            scalar2=b1T[:, t, f0 + j : f0 + j + 1],
+                            op0=ALU.mult,
+                            op1=ALU.add,
+                        )
+                grouped = work.tile([P, GROUP * B, PACK], BF16, align_bytes=64)
+                src = pre[:].rearrange("p t (c i) -> p c t i", i=RUN)
+                dst = grouped[:].rearrange("p (c i) t -> p c t i", i=RUN)
+                cut = SCALAR_COLS // RUN
+                nc.scalar.activation(out=dst[:, :cut], in_=src[:, :cut], func=ACT.Relu)
+                nc.vector.tensor_scalar_max(out=dst[:, cut:], in0=src[:, cut:], scalar1=0.0)
+
+                h_codes = work.tile([P, GROUP * B], U32, align_bytes=64)
+                h_planes = work.tile([P, GROUP * B], U8, align_bytes=64)
+                nc.vector.quantize_mx(
+                    out=h_codes[:].bitcast(FP8X4),
+                    scales=h_planes[:],
+                    in_=grouped[:].rearrange("p c t -> p (c t)"),
+                )
+
+                out_cols = slice(f0 * E, (f0 + GROUP) * E)
+                for h in range(HALVES):
+                    acc = psum.tile([P, GROUP * E], F32)
+                    for j in range(GROUP):
+                        rows = slice(j * B + h * P, j * B + (h + 1) * P)
+                        nc.tensor.matmul_mx(
+                            out=acc[:, j * E : (j + 1) * E],
+                            lhsT=h_codes[:, rows].bitcast(FP8X4),
+                            lhsT_scale=h_planes[:, rows],
+                            rhs=w2_codes[:, f0 + j, :].bitcast(FP4X4),
+                            rhs_scale=w2_planes[:, f0 + j, :],
+                            start=True,
+                            stop=True,
+                        )
+                    res = opool.tile([P, GROUP * E], F32)
+                    nc.vector.tensor_tensor(out=res[:], in0=acc[:], in1=b2_all[:, out_cols], op=ALU.add)
+                    nc.sync.dma_start(out=out[h * P : (h + 1) * P, out_cols], in_=res[:])

@@ -18,20 +18,14 @@ B, F, H, E = 256, 128, 512, 128
 PACK = 4
 HALVES = B // P
 GROUP = 4
+GROUPS = F // GROUP
 CHUNK = 16
+CHUNKS = F // CHUNK
+GROUPS_PER_CHUNK = CHUNK // GROUP
 RUN = 4
 SCALAR_COLS = GROUP * B * 7 // 8
 
 FLOPS = 2 * B * F * H * E
-
-
-def transposed_scalars(nc, psum, pool, rows, ident, name):
-    turned = psum.tile([P, PACK, F], BF16, name=name + "_ps")
-    for t in range(PACK):
-        nc.tensor.transpose(turned[:, t, :], rows[:, t:H:PACK], ident)
-    scalars = pool.tile([P, PACK, F], F32, name=name)
-    nc.vector.tensor_copy(out=scalars[:], in_=turned[:])
-    return scalars
 
 
 def tile_densefeaturenumericembedding_e_kernel(tc, x, w1, b1, w2_words, w2_scales, b2, out):
@@ -41,100 +35,152 @@ def tile_densefeaturenumericembedding_e_kernel(tc, x, w1, b1, w2_words, w2_scale
         xpool = ctx.enter_context(tc.tile_pool(name="xpool", bufs=3))
         work = ctx.enter_context(tc.tile_pool(name="work", bufs=3))
         opool = ctx.enter_context(tc.tile_pool(name="opool", bufs=4))
-        setup_psum = ctx.enter_context(tc.psum_pool(name="setup_psum", bufs=1))
+        setup_psum = ctx.enter_context(tc.psum_pool(name="setup_psum", bufs=2))
         psum = ctx.enter_context(tc.psum_pool(name="psum", bufs=4))
+        ctx.enter_context(tc.manual_schedule())
 
         x_sb = const.tile([P, HALVES, F], BF16)
-        nc.sync.dma_start(out=x_sb[:], in_=x.rearrange("(h p) f -> p h f", p=P))
         w1_sb = const.tile([P, H], BF16)
-        nc.sync.dma_start(out=w1_sb[:], in_=w1)
         b1_sb = const.tile([P, H], BF16)
-        nc.sync.dma_start(out=b1_sb[:], in_=b1)
-
         ident = const.tile([P, P], BF16)
-        make_identity(nc, ident[:])
-
         w2_planes = const.tile([P, F, E], U8, align_bytes=64)
-        nc.vector.memset(w2_planes[:].rearrange("p g n -> p (g n)").bitcast(I32), 0)
-
-        xT_ps = setup_psum.tile([P, B], BF16)
-        for h in range(HALVES):
-            nc.tensor.transpose(xT_ps[:, h * P : (h + 1) * P], x_sb[:, h, :], ident[:])
+        w2_codes = const.tile([P, F, 2 * E], U8, align_bytes=64)
+        b2_all = const.tile([P, F * E], BF16)
+        w1T = const.tile([P, PACK, F], F32)
+        b1T = const.tile([P, PACK, F], F32)
         xT_sb = const.tile([P, B], BF16)
-        nc.vector.tensor_copy(out=xT_sb[:], in_=xT_ps[:])
-        nc.sync.dma_start(
-            out=out[0:1, :].rearrange("o (f w) -> (o f) w", w=B // 2), in_=xT_sb[:].bitcast(F32)
-        )
+        b2_row = b2.rearrange("f e -> (f e)")
+        x_spread = {}
 
-        w1T = transposed_scalars(nc, setup_psum, const, w1_sb, ident[:], "w1T")
-        b1T = transposed_scalars(nc, setup_psum, const, b1_sb, ident[:], "b1T")
+        def load_weights(c):
+            feats = slice(c * CHUNK, (c + 1) * CHUNK)
+            nc.sync.dma_start(
+                out=w2_codes[:, feats, :].bitcast(I32),
+                in_=w2_words[feats].bitcast(I32).rearrange("g p w -> p g w"),
+            )
+            cols = slice(c * CHUNK * E, (c + 1) * CHUNK * E)
+            nc.sync.dma_start(out=b2_all[:, cols], in_=b2_row[cols].partition_broadcast(P))
 
+        def load_x(c):
+            words = CHUNK * B // 2
+            x_spread[c] = xpool.tile([P, CHUNK * B], BF16, name="x_spread")
+            nc.sync.dma_start(
+                out=x_spread[c][:].bitcast(F32),
+                in_=out[0, c * words : (c + 1) * words].partition_broadcast(P),
+            )
+
+        def turn(rows, scalars):
+            turned = setup_psum.tile([P, PACK, F], BF16, name="turned")
+            for t in range(PACK):
+                nc.tensor.transpose(turned[:, t, :], rows[:, t:H:PACK], ident[:])
+            nc.vector.tensor_copy(out=scalars[:], in_=turned[:])
+
+        def spread_on_chip(g):
+            spread = setup_psum.tile([P, GROUP * B], BF16, name="spread")
+            for j in range(GROUP):
+                for h in range(HALVES):
+                    f = g * GROUP + j
+                    nc.tensor.matmul(
+                        out=spread[:, j * B + h * P : j * B + (h + 1) * P],
+                        lhsT=x_sb[:, h, f : f + 1].to_broadcast([P, P]),
+                        rhs=ident[:],
+                        start=True,
+                        stop=True,
+                    )
+            nc.scalar.copy(out=x_spread[0][:, g * GROUP * B : (g + 1) * GROUP * B], in_=spread[:])
+
+        nc.sync.dma_start(out=x_sb[:], in_=x.rearrange("(h p) f -> p h f", p=P))
+        nc.sync.dma_start(out=w1_sb[:], in_=w1)
+        nc.sync.dma_start(out=b1_sb[:], in_=b1)
+        make_identity(nc, ident[:])
+        nc.vector.memset(w2_planes[:].rearrange("p g n -> p (g n)").bitcast(I32), 0)
         for q in range(4):
             nc.sync.dma_start(
                 out=w2_planes[32 * q : 32 * q + 4, :, :].bitcast(I32),
                 in_=w2_scales[:, 4 * q : 4 * q + 4, :].bitcast(I32).rearrange("g r n -> r g n"),
             )
-        w2_codes = const.tile([P, F, 2 * E], U8, align_bytes=64)
-        b2_all = const.tile([P, F * E], BF16)
-        b2_row = b2.rearrange("f e -> (f e)")
+        load_weights(0)
 
-        words = CHUNK * B // 2
-        for c in range(F // CHUNK):
-            feats = slice(c * CHUNK, (c + 1) * CHUNK)
-            xb = xpool.tile([P, words], F32)
-            nc.sync.dma_start(out=xb[:], in_=out[0, c * words : (c + 1) * words].partition_broadcast(P))
-            nc.sync.dma_start(
-                out=w2_codes[:, feats, :].bitcast(I32),
-                in_=w2_words[feats].bitcast(I32).rearrange("g p w -> p g w"),
-            )
-            nc.sync.dma_start(
-                out=b2_all[:, c * CHUNK * E : (c + 1) * CHUNK * E],
-                in_=b2_row[c * CHUNK * E : (c + 1) * CHUNK * E].partition_broadcast(P),
-            )
-            x_all = xb[:].bitcast(BF16)
+        x_spread[0] = xpool.tile([P, CHUNK * B], BF16, name="x_spread")
+        spread_on_chip(0)
+        turn(w1_sb, w1T)
+        turn(b1_sb, b1T)
+        xT_ps = setup_psum.tile([P, B], BF16, name="turned")
+        for h in range(HALVES):
+            nc.tensor.transpose(xT_ps[:, h * P : (h + 1) * P], x_sb[:, h, :], ident[:])
+        nc.vector.tensor_copy(out=xT_sb[:], in_=xT_ps[:])
+        nc.sync.dma_start(
+            out=out[0:1, :].rearrange("o (f w) -> (o f) w", w=B // 2), in_=xT_sb[:].bitcast(F32)
+        )
+        for g in range(1, GROUPS_PER_CHUNK):
+            spread_on_chip(g)
+        for c in (1, 2):
+            load_x(c)
+            load_weights(c)
 
-            for g in range(CHUNK // GROUP):
-                f0 = c * CHUNK + g * GROUP
-                pre = work.tile([P, PACK, GROUP * B], BF16)
+        pre, grouped, h_codes, h_planes, acc = {}, {}, {}, {}, {}
+
+        def affine(g):
+            pre[g] = work.tile([P, PACK, GROUP * B], BF16, name="pre")
+            x_all = x_spread[g // GROUPS_PER_CHUNK]
+            for j in range(GROUP):
+                f = g * GROUP + j
+                for t in range(PACK):
+                    nc.vector.tensor_scalar(
+                        out=pre[g][:, t, j * B : (j + 1) * B],
+                        in0=x_all[:, (f % CHUNK) * B : (f % CHUNK + 1) * B],
+                        scalar1=w1T[:, t, f : f + 1],
+                        scalar2=b1T[:, t, f : f + 1],
+                        op0=ALU.mult,
+                        op1=ALU.add,
+                    )
+
+        def regroup(g):
+            grouped[g] = work.tile([P, GROUP * B, PACK], BF16, name="grouped", align_bytes=64)
+            src = pre[g][:].rearrange("p t (c i) -> p c t i", i=RUN)
+            dst = grouped[g][:].rearrange("p (c i) t -> p c t i", i=RUN)
+            cut = SCALAR_COLS // RUN
+            nc.scalar.activation(out=dst[:, :cut], in_=src[:, :cut], func=ACT.Relu)
+            nc.vector.tensor_scalar_max(out=dst[:, cut:], in0=src[:, cut:], scalar1=0.0)
+
+        def quantise_and_multiply(g):
+            h_codes[g] = work.tile([P, GROUP * B], U32, name="h_codes", align_bytes=64)
+            h_planes[g] = work.tile([P, GROUP * B], U8, name="h_planes", align_bytes=64)
+            nc.vector.quantize_mx(
+                out=h_codes[g][:].bitcast(FP8X4),
+                scales=h_planes[g][:],
+                in_=grouped[g][:].rearrange("p c t -> p (c t)"),
+            )
+            for h in range(HALVES):
+                acc[g, h] = psum.tile([P, GROUP * E], F32, name="acc")
                 for j in range(GROUP):
-                    for t in range(PACK):
-                        nc.vector.tensor_scalar(
-                            out=pre[:, t, j * B : (j + 1) * B],
-                            in0=x_all[:, (g * GROUP + j) * B : (g * GROUP + j + 1) * B],
-                            scalar1=w1T[:, t, f0 + j : f0 + j + 1],
-                            scalar2=b1T[:, t, f0 + j : f0 + j + 1],
-                            op0=ALU.mult,
-                            op1=ALU.add,
-                        )
-                grouped = work.tile([P, GROUP * B, PACK], BF16, align_bytes=64)
-                src = pre[:].rearrange("p t (c i) -> p c t i", i=RUN)
-                dst = grouped[:].rearrange("p (c i) t -> p c t i", i=RUN)
-                cut = SCALAR_COLS // RUN
-                nc.scalar.activation(out=dst[:, :cut], in_=src[:, :cut], func=ACT.Relu)
-                nc.vector.tensor_scalar_max(out=dst[:, cut:], in0=src[:, cut:], scalar1=0.0)
+                    rows = slice(j * B + h * P, j * B + (h + 1) * P)
+                    nc.tensor.matmul_mx(
+                        out=acc[g, h][:, j * E : (j + 1) * E],
+                        lhsT=h_codes[g][:, rows].bitcast(FP8X4),
+                        lhsT_scale=h_planes[g][:, rows],
+                        rhs=w2_codes[:, g * GROUP + j, :].bitcast(FP4X4),
+                        rhs_scale=w2_planes[:, g * GROUP + j, :],
+                        start=True,
+                        stop=True,
+                    )
 
-                h_codes = work.tile([P, GROUP * B], U32, align_bytes=64)
-                h_planes = work.tile([P, GROUP * B], U8, align_bytes=64)
-                nc.vector.quantize_mx(
-                    out=h_codes[:].bitcast(FP8X4),
-                    scales=h_planes[:],
-                    in_=grouped[:].rearrange("p c t -> p (c t)"),
-                )
+        def finish(g):
+            cols = slice(g * GROUP * E, (g + 1) * GROUP * E)
+            for h in range(HALVES):
+                res = opool.tile([P, GROUP * E], F32)
+                nc.vector.tensor_tensor(out=res[:], in0=acc[g, h][:], in1=b2_all[:, cols], op=ALU.add)
+                nc.sync.dma_start(out=out[h * P : (h + 1) * P, cols], in_=res[:])
 
-                out_cols = slice(f0 * E, (f0 + GROUP) * E)
-                for h in range(HALVES):
-                    acc = psum.tile([P, GROUP * E], F32)
-                    for j in range(GROUP):
-                        rows = slice(j * B + h * P, j * B + (h + 1) * P)
-                        nc.tensor.matmul_mx(
-                            out=acc[:, j * E : (j + 1) * E],
-                            lhsT=h_codes[:, rows].bitcast(FP8X4),
-                            lhsT_scale=h_planes[:, rows],
-                            rhs=w2_codes[:, f0 + j, :].bitcast(FP4X4),
-                            rhs_scale=w2_planes[:, f0 + j, :],
-                            start=True,
-                            stop=True,
-                        )
-                    res = opool.tile([P, GROUP * E], F32)
-                    nc.vector.tensor_tensor(out=res[:], in0=acc[:], in1=b2_all[:, out_cols], op=ALU.add)
-                    nc.sync.dma_start(out=out[h * P : (h + 1) * P, out_cols], in_=res[:])
+        for step in range(GROUPS + 3):
+            if step < GROUPS:
+                affine(step)
+            if 0 <= step - 1 < GROUPS:
+                regroup(step - 1)
+            if 0 <= step - 2 < GROUPS:
+                quantise_and_multiply(step - 2)
+            if 0 <= step - 3 < GROUPS:
+                finish(step - 3)
+            if step % GROUPS_PER_CHUNK == 0 and 3 <= step // GROUPS_PER_CHUNK + 2 < CHUNKS:
+                load_x(step // GROUPS_PER_CHUNK + 2)
+                load_weights(step // GROUPS_PER_CHUNK + 2)

@@ -23,7 +23,8 @@ CHUNK = 16
 CHUNKS = F // CHUNK
 GROUPS_PER_CHUNK = CHUNK // GROUP
 RUN = 4
-SCALAR_COLS = GROUP * B * 7 // 8
+SCALAR_COLS = GROUP * B * 15 // 16
+LAST_SCALAR_COLS = GROUP * B * 3 // 8
 
 FLOPS = 2 * B * F * H * E
 
@@ -33,8 +34,8 @@ def tile_densefeaturenumericembedding_e_kernel(tc, x, w1, b1, w2_words, w2_scale
     with ExitStack() as ctx:
         const = ctx.enter_context(tc.tile_pool(name="const", bufs=1))
         xpool = ctx.enter_context(tc.tile_pool(name="xpool", bufs=3))
-        work = ctx.enter_context(tc.tile_pool(name="work", bufs=3))
-        opool = ctx.enter_context(tc.tile_pool(name="opool", bufs=4))
+        work = ctx.enter_context(tc.tile_pool(name="work", bufs=4))
+        opool = ctx.enter_context(tc.tile_pool(name="opool", bufs=8))
         setup_psum = ctx.enter_context(tc.psum_pool(name="setup_psum", bufs=2))
         psum = ctx.enter_context(tc.psum_pool(name="psum", bufs=4))
         ctx.enter_context(tc.manual_schedule())
@@ -108,7 +109,7 @@ def tile_densefeaturenumericembedding_e_kernel(tc, x, w1, b1, w2_words, w2_scale
         xT_ps = setup_psum.tile([P, B], BF16, name="turned")
         for h in range(HALVES):
             nc.tensor.transpose(xT_ps[:, h * P : (h + 1) * P], x_sb[:, h, :], ident[:])
-        nc.vector.tensor_copy(out=xT_sb[:], in_=xT_ps[:])
+        nc.scalar.copy(out=xT_sb[:], in_=xT_ps[:])
         nc.sync.dma_start(
             out=out[0:1, :].rearrange("o (f w) -> (o f) w", w=B // 2), in_=xT_sb[:].bitcast(F32)
         )
@@ -139,7 +140,7 @@ def tile_densefeaturenumericembedding_e_kernel(tc, x, w1, b1, w2_words, w2_scale
             grouped[g] = work.tile([P, GROUP * B, PACK], BF16, name="grouped", align_bytes=64)
             src = pre[g][:].rearrange("p t (c i) -> p c t i", i=RUN)
             dst = grouped[g][:].rearrange("p (c i) t -> p c t i", i=RUN)
-            cut = SCALAR_COLS // RUN
+            cut = (LAST_SCALAR_COLS if g == GROUPS - 1 else SCALAR_COLS) // RUN
             nc.scalar.activation(out=dst[:, :cut], in_=src[:, :cut], func=ACT.Relu)
             nc.vector.tensor_scalar_max(out=dst[:, cut:], in0=src[:, cut:], scalar1=0.0)
 

@@ -23,8 +23,9 @@ CHUNK = 16
 CHUNKS = F // CHUNK
 GROUPS_PER_CHUNK = CHUNK // GROUP
 RUN = 4
-SCALAR_COLS = GROUP * B * 15 // 16
+SCALAR_COLS = GROUP * B * 7 // 8
 LAST_SCALAR_COLS = GROUP * B * 3 // 8
+FLT_MAX = 3.4028234663852886e38
 
 FLOPS = 2 * B * F * H * E
 
@@ -136,13 +137,26 @@ def tile_densefeaturenumericembedding_e_kernel(tc, x, w1, b1, w2_words, w2_scale
                         op1=ALU.add,
                     )
 
-        def regroup(g):
-            grouped[g] = work.tile([P, GROUP * B, PACK], BF16, name="grouped", align_bytes=64)
+        def regroup_views(g):
             src = pre[g][:].rearrange("p t (c i) -> p c t i", i=RUN)
             dst = grouped[g][:].rearrange("p (c i) t -> p c t i", i=RUN)
+            return src, dst
+
+        def regroup_on_gpsimd(g):
+            grouped[g] = work.tile([P, GROUP * B, PACK], BF16, name="grouped", align_bytes=64)
+            src, dst = regroup_views(g)
+            cut = SCALAR_COLS // RUN
+            nc.gpsimd.tensor_scalar(
+                out=dst[:, cut:], in0=src[:, cut:], scalar1=FLT_MAX, scalar2=0.0, op0=ALU.min, op1=ALU.max
+            )
+
+        def regroup(g):
+            src, dst = regroup_views(g)
+            end = SCALAR_COLS // RUN
             cut = (LAST_SCALAR_COLS if g == GROUPS - 1 else SCALAR_COLS) // RUN
             nc.scalar.activation(out=dst[:, :cut], in_=src[:, :cut], func=ACT.Relu)
-            nc.vector.tensor_scalar_max(out=dst[:, cut:], in0=src[:, cut:], scalar1=0.0)
+            if cut < end:
+                nc.vector.tensor_scalar_max(out=dst[:, cut:end], in0=src[:, cut:end], scalar1=0.0)
 
         def quantise_and_multiply(g):
             h_codes[g] = work.tile([P, GROUP * B], U32, name="h_codes", align_bytes=64)
@@ -176,12 +190,13 @@ def tile_densefeaturenumericembedding_e_kernel(tc, x, w1, b1, w2_words, w2_scale
         for step in range(GROUPS + 3):
             if step < GROUPS:
                 affine(step)
+                regroup_on_gpsimd(step)
             if 0 <= step - 1 < GROUPS:
                 regroup(step - 1)
-            if 0 <= step - 2 < GROUPS:
-                quantise_and_multiply(step - 2)
             if 0 <= step - 3 < GROUPS:
                 finish(step - 3)
+            if 0 <= step - 2 < GROUPS:
+                quantise_and_multiply(step - 2)
             if step % GROUPS_PER_CHUNK == 0 and 3 <= step // GROUPS_PER_CHUNK + 2 < CHUNKS:
                 load_x(step // GROUPS_PER_CHUNK + 2)
                 load_weights(step // GROUPS_PER_CHUNK + 2)

@@ -187,14 +187,14 @@ def tile_densefeaturenumericembedding_e_kernel(tc, x, w1, b1, w2_words, w2_scale
                 nc.vector.tensor_tensor(out=res[:], in0=acc[g, h][:], in1=b2_all[:, cols], op=ALU.add)
                 nc.sync.dma_start(out=out[h * P : (h + 1) * P, cols], in_=res[:])
 
-        for step in range(GROUPS + 3):
+        for step in range(GROUPS + 4):
             if step < GROUPS:
                 affine(step)
                 regroup_on_gpsimd(step)
             if 0 <= step - 1 < GROUPS:
                 regroup(step - 1)
-            if 0 <= step - 3 < GROUPS:
-                finish(step - 3)
+            if 0 <= step - 4 < GROUPS:
+                finish(step - 4)
             if 0 <= step - 2 < GROUPS:
                 quantise_and_multiply(step - 2)
             if step % GROUPS_PER_CHUNK == 0 and 3 <= step // GROUPS_PER_CHUNK + 2 < CHUNKS:

@@ -26,6 +26,7 @@ RUN = 4
 SCALAR_COLS = GROUP * B * 7 // 8
 LAST_SCALAR_COLS = GROUP * B * 3 // 8
 FLT_MAX = 3.4028234663852886e38
+GPSIMD_LEAD = 2
 
 FLOPS = 2 * B * F * H * E
 
@@ -125,17 +126,18 @@ def tile_densefeaturenumericembedding_e_kernel(tc, x, w1, b1, w2_words, w2_scale
         def affine(g):
             pre[g] = work.tile([P, PACK, GROUP * B], BF16, name="pre")
             x_all = x_spread[g // GROUPS_PER_CHUNK]
-            for j in range(GROUP):
+            planes = [(j, t) for j in range(GROUP) for t in range(PACK)]
+            planes = planes[: -PACK - GPSIMD_LEAD] + planes[-PACK:] + planes[-PACK - GPSIMD_LEAD : -PACK]
+            for j, t in planes:
                 f = g * GROUP + j
-                for t in range(PACK):
-                    nc.vector.tensor_scalar(
-                        out=pre[g][:, t, j * B : (j + 1) * B],
-                        in0=x_all[:, (f % CHUNK) * B : (f % CHUNK + 1) * B],
-                        scalar1=w1T[:, t, f : f + 1],
-                        scalar2=b1T[:, t, f : f + 1],
-                        op0=ALU.mult,
-                        op1=ALU.add,
-                    )
+                nc.vector.tensor_scalar(
+                    out=pre[g][:, t, j * B : (j + 1) * B],
+                    in0=x_all[:, (f % CHUNK) * B : (f % CHUNK + 1) * B],
+                    scalar1=w1T[:, t, f : f + 1],
+                    scalar2=b1T[:, t, f : f + 1],
+                    op0=ALU.mult,
+                    op1=ALU.add,
+                )
 
         def regroup_views(g):
             src = pre[g][:].rearrange("p t (c i) -> p c t i", i=RUN)

@@ -22,7 +22,8 @@ GROUPS = F // GROUP
 CHUNK = 16
 CHUNKS = F // CHUNK
 GROUPS_PER_CHUNK = CHUNK // GROUP
-RUN = 4
+RUN = 2
+GPSIMD_RUN = 4
 SCALAR_COLS = GROUP * B * 7 // 8
 LAST_SCALAR_COLS = GROUP * B * 3 // 8
 FLT_MAX = 3.4028234663852886e38
@@ -139,21 +140,21 @@ def tile_densefeaturenumericembedding_e_kernel(tc, x, w1, b1, w2_words, w2_scale
                     op1=ALU.add,
                 )
 
-        def regroup_views(g):
-            src = pre[g][:].rearrange("p t (c i) -> p c t i", i=RUN)
-            dst = grouped[g][:].rearrange("p (c i) t -> p c t i", i=RUN)
+        def regroup_views(g, run):
+            src = pre[g][:].rearrange("p t (c i) -> p c t i", i=run)
+            dst = grouped[g][:].rearrange("p (c i) t -> p c t i", i=run)
             return src, dst
 
         def regroup_on_gpsimd(g):
             grouped[g] = work.tile([P, GROUP * B, PACK], BF16, name="grouped", align_bytes=64)
-            src, dst = regroup_views(g)
-            cut = SCALAR_COLS // RUN
+            src, dst = regroup_views(g, GPSIMD_RUN)
+            cut = SCALAR_COLS // GPSIMD_RUN
             nc.gpsimd.tensor_scalar(
                 out=dst[:, cut:], in0=src[:, cut:], scalar1=FLT_MAX, scalar2=0.0, op0=ALU.min, op1=ALU.max
             )
 
         def regroup(g):
-            src, dst = regroup_views(g)
+            src, dst = regroup_views(g, RUN)
             end = SCALAR_COLS // RUN
             cut = (LAST_SCALAR_COLS if g == GROUPS - 1 else SCALAR_COLS) // RUN
             nc.scalar.activation(out=dst[:, :cut], in_=src[:, :cut], func=ACT.Relu)

@@ -12,6 +12,7 @@ FP8X4 = mybir.dt.float8_e4m3fn_x4
 FP4X4 = mybir.dt.float4_e2m1fn_x4
 ALU = mybir.AluOpType
 ACT = mybir.ActivationFunctionType
+AX = mybir.AxisListType
 
 P = 128
 B, F, H, E = 256, 128, 512, 128
@@ -28,6 +29,11 @@ SCALAR_COLS = GROUP * B * 7 // 8
 LAST_SCALAR_COLS = GROUP * B * 3 // 8
 FLT_MAX = 3.4028234663852886e38
 GPSIMD_LEAD = 2
+
+PLAIN_GROUPS = range(8, GROUPS, 2)
+PLAIN = len(PLAIN_GROUPS)
+PLAIN_FEATURES = slice(PLAIN_GROUPS.start * GROUP, F, PLAIN_GROUPS.step * GROUP)
+SLOTS = 16
 
 FLOPS = 2 * B * F * H * E
 
@@ -53,6 +59,14 @@ def tile_densefeaturenumericembedding_e_kernel(tc, x, w1, b1, w2_words, w2_scale
         w1T = const.tile([P, PACK, F], F32)
         b1T = const.tile([P, PACK, F], F32)
         xT_sb = const.tile([P, B], BF16)
+        w_cols = const.tile([P, 2, PACK, SLOTS], BF16)
+        w_rows = const.tile([P, P], BF16)
+        w_picked = const.tile([P, PLAIN, P], BF16)
+        x_cols = const.tile([P, HALVES, 2, PACK, SLOTS], BF16)
+        x_rows = const.tile([P, B], BF16)
+        x_wide = const.tile([P, B, PACK], BF16)
+        pick = const.tile([P, SLOTS], F32)
+        pick_t = const.tile([P, PACK], F32)
         b2_row = b2.rearrange("f e -> (f e)")
         x_spread = {}
 
@@ -84,12 +98,10 @@ def tile_densefeaturenumericembedding_e_kernel(tc, x, w1, b1, w2_words, w2_scale
             for j in range(GROUP):
                 for h in range(HALVES):
                     f = g * GROUP + j
-                    nc.tensor.matmul(
-                        out=spread[:, j * B + h * P : j * B + (h + 1) * P],
-                        lhsT=x_sb[:, h, f : f + 1].to_broadcast([P, P]),
-                        rhs=ident[:],
-                        start=True,
-                        stop=True,
+                    nc.tensor.transpose(
+                        spread[:, j * B + h * P : j * B + (h + 1) * P],
+                        x_sb[:, h, f : f + 1].to_broadcast([P, P]),
+                        ident[:],
                     )
             nc.scalar.copy(out=x_spread[0][:, g * GROUP * B : (g + 1) * GROUP * B], in_=spread[:])
 
@@ -97,6 +109,8 @@ def tile_densefeaturenumericembedding_e_kernel(tc, x, w1, b1, w2_words, w2_scale
         nc.sync.dma_start(out=w1_sb[:], in_=w1)
         nc.sync.dma_start(out=b1_sb[:], in_=b1)
         make_identity(nc, ident[:])
+        nc.gpsimd.memset(x_cols[:], 1.0)
+        nc.gpsimd.memset(w_cols[:], 0.0)
         nc.vector.memset(w2_planes[:].rearrange("p g n -> p (g n)").bitcast(I32), 0)
         for q in range(4):
             nc.sync.dma_start(
@@ -104,6 +118,17 @@ def tile_densefeaturenumericembedding_e_kernel(tc, x, w1, b1, w2_words, w2_scale
                 in_=w2_scales[:, 4 * q : 4 * q + 4, :].bitcast(I32).rearrange("g r n -> r g n"),
             )
         load_weights(0)
+        nc.vector.tensor_reduce(
+            out=pick[:], in_=ident[:].rearrange("r (m i) -> r i m", i=SLOTS), axis=AX.X, op=ALU.add
+        )
+        nc.vector.tensor_reduce(
+            out=pick_t[:], in_=ident[:].rearrange("r (s t i) -> r t s i", s=2, t=PACK), axis=AX.XY, op=ALU.add
+        )
+        for h in range(HALVES):
+            nc.gpsimd.tensor_copy(
+                out=x_cols[:, h, 0, :, :PLAIN],
+                in_=x_sb[:, h, PLAIN_FEATURES].unsqueeze(1).to_broadcast([P, PACK, PLAIN]),
+            )
 
         x_spread[0] = xpool.tile([P, CHUNK * B], BF16, name="x_spread")
         spread_on_chip(0)
@@ -113,21 +138,54 @@ def tile_densefeaturenumericembedding_e_kernel(tc, x, w1, b1, w2_words, w2_scale
         for h in range(HALVES):
             nc.tensor.transpose(xT_ps[:, h * P : (h + 1) * P], x_sb[:, h, :], ident[:])
         nc.scalar.copy(out=xT_sb[:], in_=xT_ps[:])
+        x_rows_ps = setup_psum.tile([P, B], BF16, name="turned")
+        for h in range(HALVES):
+            nc.tensor.transpose(
+                x_rows_ps[:, h * P : (h + 1) * P], x_cols[:, h].rearrange("p s t i -> p (s t i)"), ident[:]
+            )
+        nc.scalar.copy(out=x_rows[:], in_=x_rows_ps[:])
+        nc.gpsimd.tensor_tensor(
+            out=x_wide[:],
+            in0=x_rows[:].unsqueeze(2).to_broadcast([P, B, PACK]),
+            in1=pick_t[:].unsqueeze(1).to_broadcast([P, B, PACK]),
+            op=ALU.mult,
+        )
+        for s, scalars in enumerate((w1T, b1T)):
+            nc.gpsimd.tensor_copy(out=w_cols[:, s, :, :PLAIN], in_=scalars[:, :, PLAIN_FEATURES])
         nc.sync.dma_start(
             out=out[0:1, :].rearrange("o (f w) -> (o f) w", w=B // 2), in_=xT_sb[:].bitcast(F32)
         )
         for g in range(1, GROUPS_PER_CHUNK):
             spread_on_chip(g)
+        w_rows_ps = setup_psum.tile([P, P], BF16, name="turned")
+        nc.tensor.transpose(w_rows_ps[:], w_cols[:].rearrange("p s t i -> p (s t i)"), ident[:])
+        nc.scalar.copy(out=w_rows[:], in_=w_rows_ps[:])
         for c in (1, 2):
             load_x(c)
             load_weights(c)
 
-        pre, grouped, h_codes, h_planes, acc = {}, {}, {}, {}, {}
+        pre, grouped, h_codes, h_planes, acc, h_plain = {}, {}, {}, {}, {}, {}
+
+        def pick_plain(g):
+            i = PLAIN_GROUPS.index(g)
+            nc.scalar.activation(out=w_picked[:, i, :], in_=w_rows[:], func=ACT.Copy, scale=pick[:, i : i + 1])
+
+        def affine_on_tensor(g):
+            h_plain[g] = setup_psum.tile([P, B, PACK], BF16, name="spread")
+            for h in range(HALVES):
+                rows = slice(h * P, (h + 1) * P)
+                nc.tensor.matmul(
+                    out=h_plain[g][:, rows, :].rearrange("p b t -> p (b t)"),
+                    lhsT=w_picked[:, PLAIN_GROUPS.index(g), :],
+                    rhs=x_wide[:, rows, :].rearrange("p b t -> p (b t)"),
+                    start=True,
+                    stop=True,
+                )
 
         def affine(g):
             pre[g] = work.tile([P, PACK, GROUP * B], BF16, name="pre")
             x_all = x_spread[g // GROUPS_PER_CHUNK]
-            planes = [(j, t) for j in range(GROUP) for t in range(PACK)]
+            planes = [(j, t) for j in range(1 if g in PLAIN_GROUPS else 0, GROUP) for t in range(PACK)]
             planes = planes[: -PACK - GPSIMD_LEAD] + planes[-PACK:] + planes[-PACK - GPSIMD_LEAD : -PACK]
             for j, t in planes:
                 f = g * GROUP + j
@@ -157,7 +215,11 @@ def tile_densefeaturenumericembedding_e_kernel(tc, x, w1, b1, w2_words, w2_scale
             src, dst = regroup_views(g, RUN)
             end = SCALAR_COLS // RUN
             cut = (LAST_SCALAR_COLS if g == GROUPS - 1 else SCALAR_COLS) // RUN
-            nc.scalar.activation(out=dst[:, :cut], in_=src[:, :cut], func=ACT.Relu)
+            begin = 0
+            if g in PLAIN_GROUPS:
+                begin = B // RUN
+                nc.scalar.activation(out=grouped[g][:, :B, :], in_=h_plain[g][:], func=ACT.Relu)
+            nc.scalar.activation(out=dst[:, begin:cut], in_=src[:, begin:cut], func=ACT.Relu)
             if cut < end:
                 nc.vector.tensor_scalar_max(out=dst[:, cut:end], in0=src[:, cut:end], scalar1=0.0)
 
@@ -191,6 +253,10 @@ def tile_densefeaturenumericembedding_e_kernel(tc, x, w1, b1, w2_words, w2_scale
                 nc.sync.dma_start(out=out[h * P : (h + 1) * P, cols], in_=res[:])
 
         for step in range(GROUPS + 4):
+            if step + 2 in PLAIN_GROUPS:
+                pick_plain(step + 2)
+            if step in PLAIN_GROUPS:
+                affine_on_tensor(step)
             if step < GROUPS:
                 affine(step)
                 regroup_on_gpsimd(step)

@@ -25,7 +25,7 @@ CHUNKS = F // CHUNK
 GROUPS_PER_CHUNK = CHUNK // GROUP
 RUN = 2
 GPSIMD_RUN = 4
-SCALAR_COLS = GROUP * B * 7 // 8
+SCALAR_COLS = GROUP * B * 55 // 64
 LAST_SCALAR_COLS = GROUP * B * 3 // 8
 FLT_MAX = 3.4028234663852886e38
 GPSIMD_LEAD = 2
@@ -118,12 +118,6 @@ def tile_densefeaturenumericembedding_e_kernel(tc, x, w1, b1, w2_words, w2_scale
                 in_=w2_scales[:, 4 * q : 4 * q + 4, :].bitcast(I32).rearrange("g r n -> r g n"),
             )
         load_weights(0)
-        nc.vector.tensor_reduce(
-            out=pick[:], in_=ident[:].rearrange("r (m i) -> r i m", i=SLOTS), axis=AX.X, op=ALU.add
-        )
-        nc.vector.tensor_reduce(
-            out=pick_t[:], in_=ident[:].rearrange("r (s t i) -> r t s i", s=2, t=PACK), axis=AX.XY, op=ALU.add
-        )
         for h in range(HALVES):
             nc.gpsimd.tensor_copy(
                 out=x_cols[:, h, 0, :, :PLAIN],
@@ -138,37 +132,50 @@ def tile_densefeaturenumericembedding_e_kernel(tc, x, w1, b1, w2_words, w2_scale
         for h in range(HALVES):
             nc.tensor.transpose(xT_ps[:, h * P : (h + 1) * P], x_sb[:, h, :], ident[:])
         nc.scalar.copy(out=xT_sb[:], in_=xT_ps[:])
-        x_rows_ps = setup_psum.tile([P, B], BF16, name="turned")
-        for h in range(HALVES):
-            nc.tensor.transpose(
-                x_rows_ps[:, h * P : (h + 1) * P], x_cols[:, h].rearrange("p s t i -> p (s t i)"), ident[:]
-            )
-        nc.scalar.copy(out=x_rows[:], in_=x_rows_ps[:])
-        nc.gpsimd.tensor_tensor(
-            out=x_wide[:],
-            in0=x_rows[:].unsqueeze(2).to_broadcast([P, B, PACK]),
-            in1=pick_t[:].unsqueeze(1).to_broadcast([P, B, PACK]),
-            op=ALU.mult,
-        )
-        for s, scalars in enumerate((w1T, b1T)):
-            nc.gpsimd.tensor_copy(out=w_cols[:, s, :, :PLAIN], in_=scalars[:, :, PLAIN_FEATURES])
         nc.sync.dma_start(
             out=out[0:1, :].rearrange("o (f w) -> (o f) w", w=B // 2), in_=xT_sb[:].bitcast(F32)
         )
         for g in range(1, GROUPS_PER_CHUNK):
             spread_on_chip(g)
-        w_rows_ps = setup_psum.tile([P, P], BF16, name="turned")
-        nc.tensor.transpose(w_rows_ps[:], w_cols[:].rearrange("p s t i -> p (s t i)"), ident[:])
-        nc.scalar.copy(out=w_rows[:], in_=w_rows_ps[:])
         for c in (1, 2):
             load_x(c)
             load_weights(c)
 
         pre, grouped, h_codes, h_planes, acc, h_plain = {}, {}, {}, {}, {}, {}
 
-        def pick_plain(g):
-            i = PLAIN_GROUPS.index(g)
-            nc.scalar.activation(out=w_picked[:, i, :], in_=w_rows[:], func=ACT.Copy, scale=pick[:, i : i + 1])
+        turned_rows = {}
+
+        def turn_rows():
+            nc.vector.tensor_reduce(
+                out=pick[:], in_=ident[:].rearrange("r (m i) -> r i m", i=SLOTS), axis=AX.X, op=ALU.add
+            )
+            nc.vector.tensor_reduce(
+                out=pick_t[:], in_=ident[:].rearrange("r (s t i) -> r t s i", s=2, t=PACK), axis=AX.XY, op=ALU.add
+            )
+            for s, scalars in enumerate((w1T, b1T)):
+                nc.vector.tensor_copy(out=w_cols[:, s, :, :PLAIN], in_=scalars[:, :, PLAIN_FEATURES])
+            turned_rows["x"] = setup_psum.tile([P, B], BF16, name="turned")
+            for h in range(HALVES):
+                nc.tensor.transpose(
+                    turned_rows["x"][:, h * P : (h + 1) * P], x_cols[:, h].rearrange("p s t i -> p (s t i)"), ident[:]
+                )
+            turned_rows["w"] = setup_psum.tile([P, P], BF16, name="turned")
+            nc.tensor.transpose(turned_rows["w"][:], w_cols[:].rearrange("p s t i -> p (s t i)"), ident[:])
+
+        def widen_x():
+            nc.vector.tensor_copy(out=w_rows[:], in_=turned_rows["w"][:])
+            nc.vector.tensor_tensor(
+                out=x_wide[:],
+                in0=turned_rows["x"][:].unsqueeze(2).to_broadcast([P, B, PACK]),
+                in1=pick_t[:].unsqueeze(1).to_broadcast([P, B, PACK]),
+                op=ALU.mult,
+            )
+
+        def pick_weights():
+            for i in range(PLAIN):
+                nc.vector.tensor_scalar_mul(out=w_picked[:, i, :], in0=w_rows[:], scalar1=pick[:, i : i + 1])
+
+        prepare_plain = {1: turn_rows, 2: widen_x, 3: pick_weights}
 
         def affine_on_tensor(g):
             h_plain[g] = setup_psum.tile([P, B, PACK], BF16, name="spread")
@@ -253,13 +260,13 @@ def tile_densefeaturenumericembedding_e_kernel(tc, x, w1, b1, w2_words, w2_scale
                 nc.sync.dma_start(out=out[h * P : (h + 1) * P, cols], in_=res[:])
 
         for step in range(GROUPS + 4):
-            if step + 2 in PLAIN_GROUPS:
-                pick_plain(step + 2)
             if step in PLAIN_GROUPS:
                 affine_on_tensor(step)
             if step < GROUPS:
                 affine(step)
                 regroup_on_gpsimd(step)
+            if step in prepare_plain:
+                prepare_plain[step]()
             if 0 <= step - 1 < GROUPS:
                 regroup(step - 1)
             if 0 <= step - 4 < GROUPS:

@@ -260,8 +260,8 @@ def tile_densefeaturenumericembedding_e_kernel(tc, x, w1, b1, w2_words, w2_scale
                 nc.sync.dma_start(out=out[h * P : (h + 1) * P, cols], in_=res[:])
 
         for step in range(GROUPS + 4):
-            if step in PLAIN_GROUPS:
-                affine_on_tensor(step)
+            if step + 1 in PLAIN_GROUPS:
+                affine_on_tensor(step + 1)
             if step < GROUPS:
                 affine(step)
                 regroup_on_gpsimd(step)

@@ -44,7 +44,7 @@ def tile_densefeaturenumericembedding_e_kernel(tc, x, w1, b1, w2_words, w2_scale
         const = ctx.enter_context(tc.tile_pool(name="const", bufs=1))
         xpool = ctx.enter_context(tc.tile_pool(name="xpool", bufs=3))
         work = ctx.enter_context(tc.tile_pool(name="work", bufs=4))
-        opool = ctx.enter_context(tc.tile_pool(name="opool", bufs=8))
+        opool = ctx.enter_context(tc.tile_pool(name="opool", bufs=3))
         setup_psum = ctx.enter_context(tc.psum_pool(name="setup_psum", bufs=2))
         psum = ctx.enter_context(tc.psum_pool(name="psum", bufs=4))
         ctx.enter_context(tc.manual_schedule())
@@ -141,7 +141,7 @@ def tile_densefeaturenumericembedding_e_kernel(tc, x, w1, b1, w2_words, w2_scale
             load_x(c)
             load_weights(c)
 
-        pre, grouped, h_codes, h_planes, acc, h_plain = {}, {}, {}, {}, {}, {}
+        pre, grouped, h_codes, h_planes, acc, h_plain, results = {}, {}, {}, {}, {}, {}, {}
 
         turned_rows = {}
 
@@ -254,10 +254,17 @@ def tile_densefeaturenumericembedding_e_kernel(tc, x, w1, b1, w2_words, w2_scale
 
         def finish(g):
             cols = slice(g * GROUP * E, (g + 1) * GROUP * E)
+            place = slice(g % 2 * GROUP * E, (g % 2 + 1) * GROUP * E)
+            if g % 2 == 0:
+                results[g // 2] = opool.tile([P, HALVES, 2 * GROUP * E], F32, name="res")
+            res = results[g // 2]
             for h in range(HALVES):
-                res = opool.tile([P, GROUP * E], F32)
-                nc.vector.tensor_tensor(out=res[:], in0=acc[g, h][:], in1=b2_all[:, cols], op=ALU.add)
-                nc.sync.dma_start(out=out[h * P : (h + 1) * P, cols], in_=res[:])
+                nc.vector.tensor_tensor(out=res[:, h, place], in0=acc[g, h][:], in1=b2_all[:, cols], op=ALU.add)
+                if g >= GROUPS - 2:
+                    nc.sync.dma_start(out=out[h * P : (h + 1) * P, cols], in_=res[:, h, place])
+            if g % 2 == 1 and g < GROUPS - 2:
+                pair = slice((g - 1) * GROUP * E, (g + 1) * GROUP * E)
+                nc.sync.dma_start(out=out[:, pair].rearrange("(h p) c -> p h c", p=P), in_=res[:])
 
         for step in range(GROUPS + 4):
             if step + 1 in PLAIN_GROUPS:

@@ -56,8 +56,8 @@ def tile_densefeaturenumericembedding_e_kernel(tc, x, w1, b1, w2_words, w2_scale
         w2_planes = const.tile([P, F, E], U8, align_bytes=64)
         w2_codes = const.tile([P, F, 2 * E], U8, align_bytes=64)
         b2_all = const.tile([P, F * E], BF16)
-        w1T = const.tile([P, PACK, F], F32)
-        b1T = const.tile([P, PACK, F], F32)
+        w1T = const.tile([P, PACK, F], BF16)
+        b1T = const.tile([P, PACK, F], BF16)
         xT_sb = const.tile([P, B], BF16)
         w_cols = const.tile([P, 2, PACK, SLOTS], BF16)
         w_rows = const.tile([P, P], BF16)
@@ -93,17 +93,16 @@ def tile_densefeaturenumericembedding_e_kernel(tc, x, w1, b1, w2_words, w2_scale
                 nc.tensor.transpose(turned[:, t, :], rows[:, t:H:PACK], ident[:])
             nc.vector.tensor_copy(out=scalars[:], in_=turned[:])
 
-        def spread_on_chip(g):
-            spread = setup_psum.tile([P, GROUP * B], BF16, name="spread")
-            for j in range(GROUP):
+        def spread_on_chip(features):
+            spread = setup_psum.tile([P, len(features), B], BF16, name="spread")
+            for j, f in enumerate(features):
                 for h in range(HALVES):
-                    f = g * GROUP + j
                     nc.tensor.transpose(
-                        spread[:, j * B + h * P : j * B + (h + 1) * P],
-                        x_sb[:, h, f : f + 1].to_broadcast([P, P]),
-                        ident[:],
+                        spread[:, j, h * P : (h + 1) * P], x_sb[:, h, f : f + 1].to_broadcast([P, P]), ident[:]
                     )
-            nc.scalar.copy(out=x_spread[0][:, g * GROUP * B : (g + 1) * GROUP * B], in_=spread[:])
+            nc.scalar.copy(
+                out=x_spread[0][:, features[0] * B : (features[-1] + 1) * B], in_=spread[:].rearrange("p j b -> p (j b)")
+            )
 
         nc.sync.dma_start(out=x_sb[:], in_=x.rearrange("(h p) f -> p h f", p=P))
         nc.sync.dma_start(out=w1_sb[:], in_=w1)
@@ -112,11 +111,6 @@ def tile_densefeaturenumericembedding_e_kernel(tc, x, w1, b1, w2_words, w2_scale
         nc.gpsimd.memset(x_cols[:], 1.0)
         nc.gpsimd.memset(w_cols[:], 0.0)
         nc.vector.memset(w2_planes[:].rearrange("p g n -> p (g n)").bitcast(I32), 0)
-        for q in range(4):
-            nc.sync.dma_start(
-                out=w2_planes[32 * q : 32 * q + 4, :, :].bitcast(I32),
-                in_=w2_scales[:, 4 * q : 4 * q + 4, :].bitcast(I32).rearrange("g r n -> r g n"),
-            )
         load_weights(0)
         for h in range(HALVES):
             nc.gpsimd.tensor_copy(
@@ -125,9 +119,10 @@ def tile_densefeaturenumericembedding_e_kernel(tc, x, w1, b1, w2_words, w2_scale
             )
 
         x_spread[0] = xpool.tile([P, CHUNK * B], BF16, name="x_spread")
-        spread_on_chip(0)
+        spread_on_chip(range(1))
         turn(w1_sb, w1T)
         turn(b1_sb, b1T)
+        spread_on_chip(range(1, GROUP))
         xT_ps = setup_psum.tile([P, B], BF16, name="turned")
         for h in range(HALVES):
             nc.tensor.transpose(xT_ps[:, h * P : (h + 1) * P], x_sb[:, h, :], ident[:])
@@ -135,8 +130,13 @@ def tile_densefeaturenumericembedding_e_kernel(tc, x, w1, b1, w2_words, w2_scale
         nc.sync.dma_start(
             out=out[0:1, :].rearrange("o (f w) -> (o f) w", w=B // 2), in_=xT_sb[:].bitcast(F32)
         )
+        for q in range(4):
+            nc.sync.dma_start(
+                out=w2_planes[32 * q : 32 * q + 4, :, :].bitcast(I32),
+                in_=w2_scales[:, 4 * q : 4 * q + 4, :].bitcast(I32).rearrange("g r n -> r g n"),
+            )
         for g in range(1, GROUPS_PER_CHUNK):
-            spread_on_chip(g)
+            spread_on_chip(range(g * GROUP, (g + 1) * GROUP))
         for c in (1, 2):
             load_x(c)
             load_weights(c)
@@ -233,24 +233,28 @@ def tile_densefeaturenumericembedding_e_kernel(tc, x, w1, b1, w2_words, w2_scale
         def quantise_and_multiply(g):
             h_codes[g] = work.tile([P, GROUP * B], U32, name="h_codes", align_bytes=64)
             h_planes[g] = work.tile([P, GROUP * B], U8, name="h_planes", align_bytes=64)
-            nc.vector.quantize_mx(
-                out=h_codes[g][:].bitcast(FP8X4),
-                scales=h_planes[g][:],
-                in_=grouped[g][:].rearrange("p c t -> p (c t)"),
-            )
             for h in range(HALVES):
                 acc[g, h] = psum.tile([P, GROUP * E], F32, name="acc")
-                for j in range(GROUP):
-                    rows = slice(j * B + h * P, j * B + (h + 1) * P)
-                    nc.tensor.matmul_mx(
-                        out=acc[g, h][:, j * E : (j + 1) * E],
-                        lhsT=h_codes[g][:, rows].bitcast(FP8X4),
-                        lhsT_scale=h_planes[g][:, rows],
-                        rhs=w2_codes[:, g * GROUP + j, :].bitcast(FP4X4),
-                        rhs_scale=w2_planes[:, g * GROUP + j, :],
-                        start=True,
-                        stop=True,
-                    )
+            features = GROUP // 2 if g == GROUPS - 1 else GROUP
+            for first in range(0, GROUP, features):
+                cols = slice(first * B, (first + features) * B)
+                nc.vector.quantize_mx(
+                    out=h_codes[g][:, cols].bitcast(FP8X4),
+                    scales=h_planes[g][:, cols],
+                    in_=grouped[g][:, cols, :].rearrange("p c t -> p (c t)"),
+                )
+                for h in range(HALVES):
+                    for j in range(first, first + features):
+                        rows = slice(j * B + h * P, j * B + (h + 1) * P)
+                        nc.tensor.matmul_mx(
+                            out=acc[g, h][:, j * E : (j + 1) * E],
+                            lhsT=h_codes[g][:, rows].bitcast(FP8X4),
+                            lhsT_scale=h_planes[g][:, rows],
+                            rhs=w2_codes[:, g * GROUP + j, :].bitcast(FP4X4),
+                            rhs_scale=w2_planes[:, g * GROUP + j, :],
+                            start=True,
+                            stop=True,
+                        )
 
         def finish(g):
             cols = slice(g * GROUP * E, (g + 1) * GROUP * E)

@@ -87,6 +87,13 @@ def tile_densefeaturenumericembedding_e_kernel(tc, x, w1, b1, w2_words, w2_scale
                 in_=out[0, c * words : (c + 1) * words].partition_broadcast(P),
             )
 
+        def load_scales(features):
+            for q in range(4):
+                nc.sync.dma_start(
+                    out=w2_planes[32 * q : 32 * q + 4, features, :].bitcast(I32),
+                    in_=w2_scales[features, 4 * q : 4 * q + 4, :].bitcast(I32).rearrange("g r n -> r g n"),
+                )
+
         def turn(rows, scalars):
             turned = setup_psum.tile([P, PACK, F], BF16, name="turned")
             for t in range(PACK):
@@ -130,16 +137,14 @@ def tile_densefeaturenumericembedding_e_kernel(tc, x, w1, b1, w2_words, w2_scale
         nc.sync.dma_start(
             out=out[0:1, :].rearrange("o (f w) -> (o f) w", w=B // 2), in_=xT_sb[:].bitcast(F32)
         )
-        for q in range(4):
-            nc.sync.dma_start(
-                out=w2_planes[32 * q : 32 * q + 4, :, :].bitcast(I32),
-                in_=w2_scales[:, 4 * q : 4 * q + 4, :].bitcast(I32).rearrange("g r n -> r g n"),
-            )
+        load_scales(slice(0, 2 * CHUNK))
         for g in range(1, GROUPS_PER_CHUNK):
             spread_on_chip(range(g * GROUP, (g + 1) * GROUP))
-        for c in (1, 2):
-            load_x(c)
-            load_weights(c)
+        load_x(1)
+        load_weights(1)
+        load_x(2)
+        load_scales(slice(2 * CHUNK, F))
+        load_weights(2)
 
         pre, grouped, h_codes, h_planes, acc, h_plain, results = {}, {}, {}, {}, {}, {}, {}
 

from contextlib import ExitStack

import concourse.mybir as mybir
from concourse.masks import make_identity

BF16 = mybir.dt.bfloat16
F32 = mybir.dt.float32
I32 = mybir.dt.int32
U8 = mybir.dt.uint8
U32 = mybir.dt.uint32
FP8X4 = mybir.dt.float8_e4m3fn_x4
FP4X4 = mybir.dt.float4_e2m1fn_x4
ALU = mybir.AluOpType
ACT = mybir.ActivationFunctionType
AX = mybir.AxisListType

P = 128
B, F, H, E = 256, 128, 512, 128
PACK = 4
HALVES = B // P
GROUP = 4
GROUPS = F // GROUP
CHUNK = 16
CHUNKS = F // CHUNK
GROUPS_PER_CHUNK = CHUNK // GROUP
RUN = 2
GPSIMD_RUN = 4
SCALAR_COLS = GROUP * B * 55 // 64
LAST_SCALAR_COLS = GROUP * B * 3 // 8
FLT_MAX = 3.4028234663852886e38
GPSIMD_LEAD = 2

PLAIN_GROUPS = range(8, GROUPS, 2)
PLAIN = len(PLAIN_GROUPS)
PLAIN_FEATURES = slice(PLAIN_GROUPS.start * GROUP, F, PLAIN_GROUPS.step * GROUP)
SLOTS = 16

FLOPS = 2 * B * F * H * E


def tile_densefeaturenumericembedding_e_kernel(tc, x, w1, b1, w2_words, w2_scales, b2, out):
    nc = tc.nc
    with ExitStack() as ctx:
        const = ctx.enter_context(tc.tile_pool(name="const", bufs=1))
        xpool = ctx.enter_context(tc.tile_pool(name="xpool", bufs=3))
        work = ctx.enter_context(tc.tile_pool(name="work", bufs=4))
        opool = ctx.enter_context(tc.tile_pool(name="opool", bufs=3))
        setup_psum = ctx.enter_context(tc.psum_pool(name="setup_psum", bufs=2))
        psum = ctx.enter_context(tc.psum_pool(name="psum", bufs=4))
        ctx.enter_context(tc.manual_schedule())

        x_sb = const.tile([P, HALVES, F], BF16)
        w1_sb = const.tile([P, H], BF16)
        b1_sb = const.tile([P, H], BF16)
        ident = const.tile([P, P], BF16)
        w2_planes = const.tile([P, F, E], U8, align_bytes=64)
        w2_codes = const.tile([P, F, 2 * E], U8, align_bytes=64)
        b2_all = const.tile([P, F * E], BF16)
        w1T = const.tile([P, PACK, F], BF16)
        b1T = const.tile([P, PACK, F], BF16)
        xT_sb = const.tile([P, B], BF16)
        w_cols = const.tile([P, 2, PACK, SLOTS], BF16)
        w_rows = const.tile([P, P], BF16)
        w_picked = const.tile([P, PLAIN, P], BF16)
        x_cols = const.tile([P, HALVES, 2, PACK, SLOTS], BF16)
        x_rows = const.tile([P, B], BF16)
        x_wide = const.tile([P, B, PACK], BF16)
        pick = const.tile([P, SLOTS], F32)
        pick_t = const.tile([P, PACK], F32)
        b2_row = b2.rearrange("f e -> (f e)")
        x_spread = {}

        def load_weights(c):
            feats = slice(c * CHUNK, (c + 1) * CHUNK)
            nc.sync.dma_start(
                out=w2_codes[:, feats, :].bitcast(I32),
                in_=w2_words[feats].bitcast(I32).rearrange("g p w -> p g w"),
            )
            cols = slice(c * CHUNK * E, (c + 1) * CHUNK * E)
            nc.sync.dma_start(out=b2_all[:, cols], in_=b2_row[cols].partition_broadcast(P))

        def load_x(c):
            words = CHUNK * B // 2
            x_spread[c] = xpool.tile([P, CHUNK * B], BF16, name="x_spread")
            nc.sync.dma_start(
                out=x_spread[c][:].bitcast(F32),
                in_=out[0, c * words : (c + 1) * words].partition_broadcast(P),
            )

        def load_scales(features):
            for q in range(4):
                nc.sync.dma_start(
                    out=w2_planes[32 * q : 32 * q + 4, features, :].bitcast(I32),
                    in_=w2_scales[features, 4 * q : 4 * q + 4, :].bitcast(I32).rearrange("g r n -> r g n"),
                )

        def turn(rows, scalars):
            turned = setup_psum.tile([P, PACK, F], BF16, name="turned")
            for t in range(PACK):
                nc.tensor.transpose(turned[:, t, :], rows[:, t:H:PACK], ident[:])
            nc.vector.tensor_copy(out=scalars[:], in_=turned[:])

        def spread_on_chip(features):
            spread = setup_psum.tile([P, len(features), B], BF16, name="spread")
            for j, f in enumerate(features):
                for h in range(HALVES):
                    nc.tensor.transpose(
                        spread[:, j, h * P : (h + 1) * P], x_sb[:, h, f : f + 1].to_broadcast([P, P]), ident[:]
                    )
            nc.scalar.copy(
                out=x_spread[0][:, features[0] * B : (features[-1] + 1) * B], in_=spread[:].rearrange("p j b -> p (j b)")
            )

        nc.sync.dma_start(out=x_sb[:], in_=x.rearrange("(h p) f -> p h f", p=P))
        nc.sync.dma_start(out=w1_sb[:], in_=w1)
        nc.sync.dma_start(out=b1_sb[:], in_=b1)
        make_identity(nc, ident[:])
        nc.gpsimd.memset(x_cols[:], 1.0)
        nc.gpsimd.memset(w_cols[:], 0.0)
        nc.vector.memset(w2_planes[:].rearrange("p g n -> p (g n)").bitcast(I32), 0)
        load_weights(0)
        for h in range(HALVES):
            nc.gpsimd.tensor_copy(
                out=x_cols[:, h, 0, :, :PLAIN],
                in_=x_sb[:, h, PLAIN_FEATURES].unsqueeze(1).to_broadcast([P, PACK, PLAIN]),
            )

        x_spread[0] = xpool.tile([P, CHUNK * B], BF16, name="x_spread")
        spread_on_chip(range(1))
        turn(w1_sb, w1T)
        turn(b1_sb, b1T)
        spread_on_chip(range(1, GROUP))
        xT_ps = setup_psum.tile([P, B], BF16, name="turned")
        for h in range(HALVES):
            nc.tensor.transpose(xT_ps[:, h * P : (h + 1) * P], x_sb[:, h, :], ident[:])
        nc.scalar.copy(out=xT_sb[:], in_=xT_ps[:])
        nc.sync.dma_start(
            out=out[0:1, :].rearrange("o (f w) -> (o f) w", w=B // 2), in_=xT_sb[:].bitcast(F32)
        )
        load_scales(slice(0, 2 * CHUNK))
        for g in range(1, GROUPS_PER_CHUNK):
            spread_on_chip(range(g * GROUP, (g + 1) * GROUP))
        load_x(1)
        load_weights(1)
        load_x(2)
        load_scales(slice(2 * CHUNK, F))
        load_weights(2)

        pre, grouped, h_codes, h_planes, acc, h_plain, results = {}, {}, {}, {}, {}, {}, {}

        turned_rows = {}

        def turn_rows():
            nc.vector.tensor_reduce(
                out=pick[:], in_=ident[:].rearrange("r (m i) -> r i m", i=SLOTS), axis=AX.X, op=ALU.add
            )
            nc.vector.tensor_reduce(
                out=pick_t[:], in_=ident[:].rearrange("r (s t i) -> r t s i", s=2, t=PACK), axis=AX.XY, op=ALU.add
            )
            for s, scalars in enumerate((w1T, b1T)):
                nc.vector.tensor_copy(out=w_cols[:, s, :, :PLAIN], in_=scalars[:, :, PLAIN_FEATURES])
            turned_rows["x"] = setup_psum.tile([P, B], BF16, name="turned")
            for h in range(HALVES):
                nc.tensor.transpose(
                    turned_rows["x"][:, h * P : (h + 1) * P], x_cols[:, h].rearrange("p s t i -> p (s t i)"), ident[:]
                )
            turned_rows["w"] = setup_psum.tile([P, P], BF16, name="turned")
            nc.tensor.transpose(turned_rows["w"][:], w_cols[:].rearrange("p s t i -> p (s t i)"), ident[:])

        def widen_x():
            nc.vector.tensor_copy(out=w_rows[:], in_=turned_rows["w"][:])
            nc.vector.tensor_tensor(
                out=x_wide[:],
                in0=turned_rows["x"][:].unsqueeze(2).to_broadcast([P, B, PACK]),
                in1=pick_t[:].unsqueeze(1).to_broadcast([P, B, PACK]),
                op=ALU.mult,
            )

        def pick_weights():
            for i in range(PLAIN):
                nc.vector.tensor_scalar_mul(out=w_picked[:, i, :], in0=w_rows[:], scalar1=pick[:, i : i + 1])

        prepare_plain = {1: turn_rows, 2: widen_x, 3: pick_weights}

        def affine_on_tensor(g):
            h_plain[g] = setup_psum.tile([P, B, PACK], BF16, name="spread")
            for h in range(HALVES):
                rows = slice(h * P, (h + 1) * P)
                nc.tensor.matmul(
                    out=h_plain[g][:, rows, :].rearrange("p b t -> p (b t)"),
                    lhsT=w_picked[:, PLAIN_GROUPS.index(g), :],
                    rhs=x_wide[:, rows, :].rearrange("p b t -> p (b t)"),
                    start=True,
                    stop=True,
                )

        def affine(g):
            pre[g] = work.tile([P, PACK, GROUP * B], BF16, name="pre")
            x_all = x_spread[g // GROUPS_PER_CHUNK]
            planes = [(j, t) for j in range(1 if g in PLAIN_GROUPS else 0, GROUP) for t in range(PACK)]
            planes = planes[: -PACK - GPSIMD_LEAD] + planes[-PACK:] + planes[-PACK - GPSIMD_LEAD : -PACK]
            for j, t in planes:
                f = g * GROUP + j
                nc.vector.tensor_scalar(
                    out=pre[g][:, t, j * B : (j + 1) * B],
                    in0=x_all[:, (f % CHUNK) * B : (f % CHUNK + 1) * B],
                    scalar1=w1T[:, t, f : f + 1],
                    scalar2=b1T[:, t, f : f + 1],
                    op0=ALU.mult,
                    op1=ALU.add,
                )

        def regroup_views(g, run):
            src = pre[g][:].rearrange("p t (c i) -> p c t i", i=run)
            dst = grouped[g][:].rearrange("p (c i) t -> p c t i", i=run)
            return src, dst

        def regroup_on_gpsimd(g):
            grouped[g] = work.tile([P, GROUP * B, PACK], BF16, name="grouped", align_bytes=64)
            src, dst = regroup_views(g, GPSIMD_RUN)
            cut = SCALAR_COLS // GPSIMD_RUN
            nc.gpsimd.tensor_scalar(
                out=dst[:, cut:], in0=src[:, cut:], scalar1=FLT_MAX, scalar2=0.0, op0=ALU.min, op1=ALU.max
            )

        def regroup(g):
            src, dst = regroup_views(g, RUN)
            end = SCALAR_COLS // RUN
            cut = (LAST_SCALAR_COLS if g == GROUPS - 1 else SCALAR_COLS) // RUN
            begin = 0
            if g in PLAIN_GROUPS:
                begin = B // RUN
                nc.scalar.activation(out=grouped[g][:, :B, :], in_=h_plain[g][:], func=ACT.Relu)
            nc.scalar.activation(out=dst[:, begin:cut], in_=src[:, begin:cut], func=ACT.Relu)
            if cut < end:
                nc.vector.tensor_scalar_max(out=dst[:, cut:end], in0=src[:, cut:end], scalar1=0.0)

        def quantise_and_multiply(g):
            h_codes[g] = work.tile([P, GROUP * B], U32, name="h_codes", align_bytes=64)
            h_planes[g] = work.tile([P, GROUP * B], U8, name="h_planes", align_bytes=64)
            for h in range(HALVES):
                acc[g, h] = psum.tile([P, GROUP * E], F32, name="acc")
            features = GROUP // 2 if g == GROUPS - 1 else GROUP
            for first in range(0, GROUP, features):
                cols = slice(first * B, (first + features) * B)
                nc.vector.quantize_mx(
                    out=h_codes[g][:, cols].bitcast(FP8X4),
                    scales=h_planes[g][:, cols],
                    in_=grouped[g][:, cols, :].rearrange("p c t -> p (c t)"),
                )
                for h in range(HALVES):
                    for j in range(first, first + features):
                        rows = slice(j * B + h * P, j * B + (h + 1) * P)
                        nc.tensor.matmul_mx(
                            out=acc[g, h][:, j * E : (j + 1) * E],
                            lhsT=h_codes[g][:, rows].bitcast(FP8X4),
                            lhsT_scale=h_planes[g][:, rows],
                            rhs=w2_codes[:, g * GROUP + j, :].bitcast(FP4X4),
                            rhs_scale=w2_planes[:, g * GROUP + j, :],
                            start=True,
                            stop=True,
                        )

        def finish(g):
            cols = slice(g * GROUP * E, (g + 1) * GROUP * E)
            place = slice(g % 2 * GROUP * E, (g % 2 + 1) * GROUP * E)
            if g % 2 == 0:
                results[g // 2] = opool.tile([P, HALVES, 2 * GROUP * E], F32, name="res")
            res = results[g // 2]
            for h in range(HALVES):
                nc.vector.tensor_tensor(out=res[:, h, place], in0=acc[g, h][:], in1=b2_all[:, cols], op=ALU.add)
                if g >= GROUPS - 2:
                    nc.sync.dma_start(out=out[h * P : (h + 1) * P, cols], in_=res[:, h, place])
            if g % 2 == 1 and g < GROUPS - 2:
                pair = slice((g - 1) * GROUP * E, (g + 1) * GROUP * E)
                nc.sync.dma_start(out=out[:, pair].rearrange("(h p) c -> p h c", p=P), in_=res[:])

        for step in range(GROUPS + 4):
            if step + 1 in PLAIN_GROUPS:
                affine_on_tensor(step + 1)
            if step < GROUPS:
                affine(step)
                regroup_on_gpsimd(step)
            if step in prepare_plain:
                prepare_plain[step]()
            if 0 <= step - 1 < GROUPS:
                regroup(step - 1)
            if 0 <= step - 4 < GROUPS:
                finish(step - 4)
            if 0 <= step - 2 < GROUPS:
                quantise_and_multiply(step - 2)
            if step % GROUPS_PER_CHUNK == 0 and 3 <= step // GROUPS_PER_CHUNK + 2 < CHUNKS:
                load_x(step // GROUPS_PER_CHUNK + 2)
                load_weights(step // GROUPS_PER_CHUNK + 2)
